import numpy as np
import ml_dtypes


def mxq(x, axis, fmt="e4m3"):
    dtype, down = {"e4m3": (ml_dtypes.float8_e4m3fn, 7), "e5m2": (ml_dtypes.float8_e5m2, 14)}[fmt]
    v = np.moveaxis(np.asarray(x, np.float32).astype(ml_dtypes.bfloat16).astype(np.float64), axis, -1)
    blocks = v.reshape(v.shape[:-1] + (-1, 32))
    amax = np.abs(blocks).max(-1, keepdims=True)
    byte = np.maximum(np.where(amax > 0, np.frexp(amax)[1] - 1 + 127, 0) - down, 1)
    scale = np.exp2(byte - 127.0)
    codes = (blocks / scale).astype(np.float32).astype(dtype).astype(np.float64)
    return np.moveaxis((codes * scale).reshape(v.shape), -1, axis)


WIDE = False


def mx_kscale(k):
    if not WIDE:
        return np.ones(k)
    levels = np.array([10, -10, 5, -5, 0])
    a = np.random.permutation(np.resize(levels, k // 512 * 4)).reshape(k // 512, 4)
    idx = np.arange(k)
    return np.exp2(a[idx // 512, idx % 128 // 32])


BF16 = ml_dtypes.bfloat16


def bf(x):
    return np.asarray(x, np.float32).astype(BF16)


def f64(x):
    return np.asarray(x).astype(np.float64)


B, N, D, H, E, O = 8, 512, 512, 1, 1024, 2048


def setup_inputs():
    s = mx_kscale(E)
    g = np.sqrt(2.0 / np.sqrt(D)) / np.sqrt(E)
    return {"x": bf(np.random.standard_normal((B, N, E)) * s),
            "w_q": bf(np.random.standard_normal((H * D, E)) * g / s),
            "w_k": bf(np.random.standard_normal((H * D, E)) * g / s)}


def reference(x, w_q, w_k):
    xq = mxq(f64(x), 2, "e4m3")
    q = (xq @ mxq(f64(w_q), 1, "e4m3").T).reshape(B, N, H, D).transpose(0, 2, 1, 3)
    k = (xq @ mxq(f64(w_k), 1, "e4m3").T).reshape(B, N, H, D).transpose(0, 2, 1, 3)
    return mxq(q, 3, "e4m3") @ mxq(k, 2, "e4m3")

@@ -1,0 +1,164 @@
+from contextlib import ExitStack
+
+import concourse.mybir as mybir
+from concourse.masks import make_identity
+
+BF16 = mybir.dt.bfloat16
+F32 = mybir.dt.float32
+U32 = mybir.dt.uint32
+U8 = mybir.dt.uint8
+FP8X4 = mybir.dt.float8_e4m3fn_x4
+
+P = 128
+PACK = 4
+BATCH, TOKENS, MODEL, HEAD = 8, 512, 1024, 512
+CHUNKS = TOKENS // P
+PASSES = MODEL // (P * PACK)
+WORD_CHUNKS = MODEL // 2 // P
+PSUM_BANKS = 8
+
+assert TOKENS == HEAD == P * PACK
+
+FLOPS = 2 * BATCH * TOKENS * MODEL * HEAD * 2 + 2 * BATCH * TOKENS * HEAD * HEAD
+
+
+def mx_tiles(pool, name, shape):
+    codes = pool.tile(shape, U32, name=name + "_codes", align_bytes=64)
+    scales = pool.tile(shape, U8, name=name + "_scales", align_bytes=64)
+    return codes, scales
+
+
+def quantise(nc, grouped, operand, calls):
+    codes, scales = operand
+    width = grouped.shape[1] // PACK // calls
+    for i in range(calls):
+        cols = slice(i * width, (i + 1) * width)
+        nc.vector.quantize_mx(
+            out=codes[:, cols].bitcast(FP8X4),
+            scales=scales[:, cols],
+            in_=grouped[:, i * width * PACK : (i + 1) * width * PACK],
+        )
+
+
+def transpose_and_quantise(nc, psum, stage, identity, raw, operand, copy):
+    raw_words = raw[:].bitcast(F32).rearrange("p (r s v) -> p r s v", r=CHUNKS, s=WORD_CHUNKS)
+    grouped = stage.tile([P, CHUNKS * MODEL], BF16, name="rows_grouped", align_bytes=64)
+    grouped_words = grouped[:].bitcast(F32).rearrange(
+        "p (r g c u) -> p r g c u", r=CHUNKS, g=PASSES, u=2
+    )
+    for r in range(CHUNKS):
+        bank = psum.tile([P, WORD_CHUNKS, P], F32, tag="bank", name="turned")
+        for s in range(WORD_CHUNKS):
+            nc.tensor.transpose(bank[:, s, :], raw_words[:, r, s, :], identity[:])
+        copy(out=grouped_words[:, r], in_=bank[:].rearrange("p (g u) c -> p g c u", u=2))
+    quantise(nc, grouped[:], operand, calls=2)
+
+
+def mx_columns(operand, r, g):
+    codes, scales = operand
+    cols = slice((r * PASSES + g) * P, (r * PASSES + g + 1) * P)
+    return codes[:, cols].bitcast(FP8X4), scales[:, cols]
+
+
+def project(nc, psum, stage, name, stationary, moving):
+    grouped = stage.tile([P, CHUNKS * P, PACK], BF16, name=name + "_grouped", align_bytes=64)
+    for c in range(CHUNKS):
+        bank = psum.tile([P, PACK, P], F32, tag="bank", name="projected")
+        for t in range(PACK):
+            for g in range(PASSES):
+                lhsT, lhsT_scale = mx_columns(stationary, t, g)
+                rhs, rhs_scale = mx_columns(moving, c, g)
+                nc.tensor.matmul_mx(
+                    out=bank[:, t, :],
+                    lhsT=lhsT,
+                    lhsT_scale=lhsT_scale,
+                    rhs=rhs,
+                    rhs_scale=rhs_scale,
+                    start=(g == 0),
+                    stop=(g == PASSES - 1),
+                )
+        nc.scalar.copy(
+            out=grouped[:, c * P : (c + 1) * P, :], in_=bank[:].rearrange("p t w -> p w t")
+        )
+    return grouped
+
+
+def logits(nc, psum, results, q, k, out_b):
+    q_codes, q_scales = q
+    k_codes, k_scales = k
+    result = results.tile([P, CHUNKS, HEAD], F32, name="result")
+    for c in range(CHUNKS):
+        cols = slice(c * P, (c + 1) * P)
+        bank = psum.tile([P, HEAD], F32, tag="bank", name="logit_bank")
+        nc.tensor.matmul_mx(
+            out=bank[:],
+            lhsT=q_codes[:, cols].bitcast(FP8X4),
+            lhsT_scale=q_scales[:, cols],
+            rhs=k_codes[:].bitcast(FP8X4),
+            rhs_scale=k_scales[:],
+            start=True,
+            stop=True,
+        )
+        copy = nc.scalar.copy if c % 2 == 0 else nc.vector.tensor_copy
+        copy(out=result[:, c, :], in_=bank[:])
+    nc.sync.dma_start(out=out_b.rearrange("(p c) m -> p c m", c=CHUNKS), in_=result[:])
+
+
+def tile_attention_pa_t_kernel(tc, x, w_q, w_k, out):
+    nc = tc.nc
+    with ExitStack() as ctx:
+        keep = ctx.enter_context(tc.tile_pool(name="keep", bufs=1))
+        stage = ctx.enter_context(tc.tile_pool(name="stage", bufs=2))
+        results = ctx.enter_context(tc.tile_pool(name="results", bufs=3))
+        psum = ctx.enter_context(tc.psum_pool(name="psum", bufs=PSUM_BANKS))
+        ctx.enter_context(tc.manual_schedule())
+
+        wq_raw = keep.tile([P, CHUNKS * MODEL], BF16, name="wq_raw")
+        wk_raw = keep.tile([P, CHUNKS * MODEL], BF16, name="wk_raw")
+        x_raw = [keep.tile([P, CHUNKS * MODEL], BF16, name="x_raw%d" % b) for b in range(BATCH)]
+
+        def load_x(b):
+            nc.sync.dma_start(out=x_raw[b][:], in_=x[b].rearrange("(p r) e -> p (r e)", r=CHUNKS))
+
+        nc.sync.dma_start(out=wq_raw[:], in_=w_q.rearrange("(p r) e -> p (r e)", r=CHUNKS))
+        load_x(0)
+        nc.sync.dma_start(
+            out=wk_raw[:].rearrange("p (r e) -> p r e", r=CHUNKS),
+            in_=w_k.rearrange("(r p) e -> p r e", p=P),
+        )
+        for b in range(1, BATCH):
+            load_x(b)
+
+        identity = keep.tile([P, P], F32, name="identity")
+        make_identity(nc, identity[:])
+
+        def prepare_x(b):
+            operand = mx_tiles(stage, "x", [P, CHUNKS * PASSES * P])
+            transpose_and_quantise(
+                nc, psum, stage, identity, x_raw[b], operand, nc.vector.tensor_copy
+            )
+            return operand
+
+        wq_mx = mx_tiles(keep, "wq", [P, CHUNKS * PASSES * P])
+        wk_mx = mx_tiles(keep, "wk", [P, CHUNKS * PASSES * P])
+        transpose_and_quantise(nc, psum, stage, identity, wq_raw, wq_mx, nc.scalar.copy)
+        x_mx = prepare_x(0)
+        transpose_and_quantise(nc, psum, stage, identity, wk_raw, wk_mx, nc.scalar.copy)
+
+        q_grouped = project(nc, psum, stage, "q", wq_mx, x_mx)
+        q_mx = None
+        k_mx = None
+        for b in range(BATCH):
+            x_next = prepare_x(b + 1) if b + 1 < BATCH else None
+            q_before, k_before = q_mx, k_mx
+            q_mx = mx_tiles(stage, "q", [P, TOKENS])
+            quantise(nc, q_grouped[:].rearrange("p w t -> p (w t)"), q_mx, calls=1)
+            if b > 0:
+                logits(nc, psum, results, q_before, k_before, out[b - 1, 0])
+            k_grouped = project(nc, psum, stage, "k", x_mx, wk_mx)
+            k_mx = mx_tiles(stage, "k", [P, HEAD])
+            quantise(nc, k_grouped[:].rearrange("p w t -> p (w t)"), k_mx, calls=1)
+            if b + 1 < BATCH:
+                q_grouped = project(nc, psum, stage, "q", wq_mx, x_next)
+            x_mx = x_next
+        logits(nc, psum, results, q_mx, k_mx, out[BATCH - 1, 0])

@@ -28,16 +28,24 @@ def mx_tiles(pool, name, shape):
     return codes, scales
 
 
-def quantise(nc, grouped, operand, calls):
-    codes, scales = operand
-    width = grouped.shape[1] // PACK // calls
-    for i in range(calls):
-        cols = slice(i * width, (i + 1) * width)
-        nc.vector.quantize_mx(
-            out=codes[:, cols].bitcast(FP8X4),
-            scales=scales[:, cols],
-            in_=grouped[:, i * width * PACK : (i + 1) * width * PACK],
+def load_rows(nc, raw, rows, pieces):
+    raw_chunks = raw[:].rearrange("p (r e) -> p r e", r=CHUNKS)
+    step = CHUNKS // pieces
+    for first in range(0, CHUNKS, step):
+        nc.sync.dma_start(
+            out=raw_chunks[:, first : first + step, :], in_=rows[:, first : first + step, :]
         )
+
+
+def quantise(nc, grouped, operand, piece, pieces):
+    codes, scales = operand
+    width = grouped.shape[1] // PACK // pieces
+    cols = slice(piece * width, (piece + 1) * width)
+    nc.vector.quantize_mx(
+        out=codes[:, cols].bitcast(FP8X4),
+        scales=scales[:, cols],
+        in_=grouped[:, piece * width * PACK : (piece + 1) * width * PACK],
+    )
 
 
 def transpose_and_quantise(nc, psum, stage, identity, raw, operand, copy):
@@ -51,7 +59,9 @@ def transpose_and_quantise(nc, psum, stage, identity, raw, operand, copy):
         for s in range(WORD_CHUNKS):
             nc.tensor.transpose(bank[:, s, :], raw_words[:, r, s, :], identity[:])
         copy(out=grouped_words[:, r], in_=bank[:].rearrange("p (g u) c -> p g c u", u=2))
-    quantise(nc, grouped[:], operand, calls=2)
+        if r > 0:
+            quantise(nc, grouped[:], operand, r - 1, CHUNKS)
+    quantise(nc, grouped[:], operand, CHUNKS - 1, CHUNKS)
 
 
 def mx_columns(operand, r, g):
@@ -86,6 +96,7 @@ def project(nc, psum, stage, name, stationary, moving):
 def logits(nc, psum, results, q, k, out_b):
     q_codes, q_scales = q
     k_codes, k_scales = k
+    out_chunks = out_b.rearrange("(p c) m -> p c m", c=CHUNKS)
     result = results.tile([P, CHUNKS, HEAD], F32, name="result")
     for c in range(CHUNKS):
         cols = slice(c * P, (c + 1) * P)
@@ -101,7 +112,7 @@ def logits(nc, psum, results, q, k, out_b):
         )
         copy = nc.scalar.copy if c % 2 == 0 else nc.vector.tensor_copy
         copy(out=result[:, c, :], in_=bank[:])
-    nc.sync.dma_start(out=out_b.rearrange("(p c) m -> p c m", c=CHUNKS), in_=result[:])
+        nc.sync.dma_start(out=out_chunks[:, c, :], in_=result[:, c, :])
 
 
 def tile_attention_pa_t_kernel(tc, x, w_q, w_k, out):
@@ -116,18 +127,11 @@ def tile_attention_pa_t_kernel(tc, x, w_q, w_k, out):
         wq_raw = keep.tile([P, CHUNKS * MODEL], BF16, name="wq_raw")
         wk_raw = keep.tile([P, CHUNKS * MODEL], BF16, name="wk_raw")
         x_raw = [keep.tile([P, CHUNKS * MODEL], BF16, name="x_raw%d" % b) for b in range(BATCH)]
-
-        def load_x(b):
-            nc.sync.dma_start(out=x_raw[b][:], in_=x[b].rearrange("(p r) e -> p (r e)", r=CHUNKS))
-
-        nc.sync.dma_start(out=wq_raw[:], in_=w_q.rearrange("(p r) e -> p (r e)", r=CHUNKS))
-        load_x(0)
-        nc.sync.dma_start(
-            out=wk_raw[:].rearrange("p (r e) -> p r e", r=CHUNKS),
-            in_=w_k.rearrange("(r p) e -> p r e", p=P),
-        )
+        load_rows(nc, wq_raw, w_q.rearrange("(p r) e -> p r e", r=CHUNKS), CHUNKS)
+        load_rows(nc, x_raw[0], x[0].rearrange("(p r) e -> p r e", r=CHUNKS), CHUNKS)
+        load_rows(nc, wk_raw, w_k.rearrange("(r p) e -> p r e", p=P), 1)
         for b in range(1, BATCH):
-            load_x(b)
+            load_rows(nc, x_raw[b], x[b].rearrange("(p r) e -> p r e", r=CHUNKS), 1)
 
         identity = keep.tile([P, P], F32, name="identity")
         make_identity(nc, identity[:])
@@ -143,21 +147,21 @@ def tile_attention_pa_t_kernel(tc, x, w_q, w_k, out):
         wk_mx = mx_tiles(keep, "wk", [P, CHUNKS * PASSES * P])
         transpose_and_quantise(nc, psum, stage, identity, wq_raw, wq_mx, nc.scalar.copy)
         x_mx = prepare_x(0)
+        q_grouped = project(nc, psum, stage, "q", wq_mx, x_mx)
         transpose_and_quantise(nc, psum, stage, identity, wk_raw, wk_mx, nc.scalar.copy)
 
-        q_grouped = project(nc, psum, stage, "q", wq_mx, x_mx)
         q_mx = None
         k_mx = None
         for b in range(BATCH):
             x_next = prepare_x(b + 1) if b + 1 < BATCH else None
             q_before, k_before = q_mx, k_mx
             q_mx = mx_tiles(stage, "q", [P, TOKENS])
-            quantise(nc, q_grouped[:].rearrange("p w t -> p (w t)"), q_mx, calls=1)
-            if b > 0:
-                logits(nc, psum, results, q_before, k_before, out[b - 1, 0])
+            quantise(nc, q_grouped[:].rearrange("p w t -> p (w t)"), q_mx, 0, 1)
             k_grouped = project(nc, psum, stage, "k", x_mx, wk_mx)
             k_mx = mx_tiles(stage, "k", [P, HEAD])
-            quantise(nc, k_grouped[:].rearrange("p w t -> p (w t)"), k_mx, calls=1)
+            quantise(nc, k_grouped[:].rearrange("p w t -> p (w t)"), k_mx, 0, 1)
+            if b > 0:
+                logits(nc, psum, results, q_before, k_before, out[b - 1, 0])
             if b + 1 < BATCH:
                 q_grouped = project(nc, psum, stage, "q", wq_mx, x_next)
             x_mx = x_next

@@ -15,7 +15,7 @@ BATCH, TOKENS, MODEL, HEAD = 8, 512, 1024, 512
 CHUNKS = TOKENS // P
 PASSES = MODEL // (P * PACK)
 WORD_CHUNKS = MODEL // 2 // P
-PSUM_BANKS = 8
+HALF_OF_PSUM = 4
 
 assert TOKENS == HEAD == P * PACK
 
@@ -28,13 +28,9 @@ def mx_tiles(pool, name, shape):
     return codes, scales
 
 
-def load_rows(nc, raw, rows, pieces):
+def load_rows(nc, raw, rows, first, end):
     raw_chunks = raw[:].rearrange("p (r e) -> p r e", r=CHUNKS)
-    step = CHUNKS // pieces
-    for first in range(0, CHUNKS, step):
-        nc.sync.dma_start(
-            out=raw_chunks[:, first : first + step, :], in_=rows[:, first : first + step, :]
-        )
+    nc.sync.dma_start(out=raw_chunks[:, first:end, :], in_=rows[:, first:end, :])
 
 
 def quantise(nc, grouped, operand, piece, pieces):
@@ -48,20 +44,19 @@ def quantise(nc, grouped, operand, piece, pieces):
     )
 
 
-def transpose_and_quantise(nc, psum, stage, identity, raw, operand, copy):
+def turn(nc, psum, identity, raw, r):
     raw_words = raw[:].bitcast(F32).rearrange("p (r s v) -> p r s v", r=CHUNKS, s=WORD_CHUNKS)
-    grouped = stage.tile([P, CHUNKS * MODEL], BF16, name="rows_grouped", align_bytes=64)
+    bank = psum.tile([P, WORD_CHUNKS, P], F32, tag="turned", name="turned", bufs=HALF_OF_PSUM)
+    for s in range(WORD_CHUNKS):
+        nc.tensor.transpose(bank[:, s, :], raw_words[:, r, s, :], identity[:])
+    return bank
+
+
+def group_words(grouped, bank, r, copy):
     grouped_words = grouped[:].bitcast(F32).rearrange(
         "p (r g c u) -> p r g c u", r=CHUNKS, g=PASSES, u=2
     )
-    for r in range(CHUNKS):
-        bank = psum.tile([P, WORD_CHUNKS, P], F32, tag="bank", name="turned")
-        for s in range(WORD_CHUNKS):
-            nc.tensor.transpose(bank[:, s, :], raw_words[:, r, s, :], identity[:])
-        copy(out=grouped_words[:, r], in_=bank[:].rearrange("p (g u) c -> p g c u", u=2))
-        if r > 0:
-            quantise(nc, grouped[:], operand, r - 1, CHUNKS)
-    quantise(nc, grouped[:], operand, CHUNKS - 1, CHUNKS)
+    copy(out=grouped_words[:, r], in_=bank[:].rearrange("p (g u) c -> p g c u", u=2))
 
 
 def mx_columns(operand, r, g):
@@ -70,27 +65,36 @@ def mx_columns(operand, r, g):
     return codes[:, cols].bitcast(FP8X4), scales[:, cols]
 
 
-def project(nc, psum, stage, name, stationary, moving):
-    grouped = stage.tile([P, CHUNKS * P, PACK], BF16, name=name + "_grouped", align_bytes=64)
-    for c in range(CHUNKS):
-        bank = psum.tile([P, PACK, P], F32, tag="bank", name="projected")
-        for t in range(PACK):
-            for g in range(PASSES):
-                lhsT, lhsT_scale = mx_columns(stationary, t, g)
-                rhs, rhs_scale = mx_columns(moving, c, g)
-                nc.tensor.matmul_mx(
-                    out=bank[:, t, :],
-                    lhsT=lhsT,
-                    lhsT_scale=lhsT_scale,
-                    rhs=rhs,
-                    rhs_scale=rhs_scale,
-                    start=(g == 0),
-                    stop=(g == PASSES - 1),
-                )
-        nc.scalar.copy(
-            out=grouped[:, c * P : (c + 1) * P, :], in_=bank[:].rearrange("p t w -> p w t")
+def sum_bank(psum):
+    return psum.tile([P, PACK, P], F32, tag="sums", name="sums", bufs=HALF_OF_PSUM)
+
+
+def project_part(nc, bank, stationary, moving, t, c):
+    for g in range(PASSES):
+        lhsT, lhsT_scale = mx_columns(stationary, t, g)
+        rhs, rhs_scale = mx_columns(moving, c, g)
+        nc.tensor.matmul_mx(
+            out=bank[:, t, :],
+            lhsT=lhsT,
+            lhsT_scale=lhsT_scale,
+            rhs=rhs,
+            rhs_scale=rhs_scale,
+            start=(g == 0),
+            stop=(g == PASSES - 1),
         )
-    return grouped
+
+
+def round_sums(nc, grouped, bank, c):
+    nc.scalar.copy(
+        out=grouped[:, c * P : (c + 1) * P, :], in_=bank[:].rearrange("p t w -> p w t")
+    )
+
+
+def project_chunk(nc, psum, grouped, stationary, moving, c):
+    bank = sum_bank(psum)
+    for t in range(PACK):
+        project_part(nc, bank, stationary, moving, t, c)
+    round_sums(nc, grouped, bank, c)
 
 
 def logits(nc, psum, results, q, k, out_b):
@@ -100,7 +104,7 @@ def logits(nc, psum, results, q, k, out_b):
     result = results.tile([P, CHUNKS, HEAD], F32, name="result")
     for c in range(CHUNKS):
         cols = slice(c * P, (c + 1) * P)
-        bank = psum.tile([P, HEAD], F32, tag="bank", name="logit_bank")
+        bank = psum.tile([P, HEAD], F32, tag="turned", name="logit_bank", bufs=HALF_OF_PSUM)
         nc.tensor.matmul_mx(
             out=bank[:],
             lhsT=q_codes[:, cols].bitcast(FP8X4),
@@ -121,48 +125,137 @@ def tile_attention_pa_t_kernel(tc, x, w_q, w_k, out):
         keep = ctx.enter_context(tc.tile_pool(name="keep", bufs=1))
         stage = ctx.enter_context(tc.tile_pool(name="stage", bufs=2))
         results = ctx.enter_context(tc.tile_pool(name="results", bufs=3))
-        psum = ctx.enter_context(tc.psum_pool(name="psum", bufs=PSUM_BANKS))
+        psum = ctx.enter_context(tc.psum_pool(name="psum", bufs=1))
         ctx.enter_context(tc.manual_schedule())
 
         wq_raw = keep.tile([P, CHUNKS * MODEL], BF16, name="wq_raw")
         wk_raw = keep.tile([P, CHUNKS * MODEL], BF16, name="wk_raw")
         x_raw = [keep.tile([P, CHUNKS * MODEL], BF16, name="x_raw%d" % b) for b in range(BATCH)]
-        load_rows(nc, wq_raw, w_q.rearrange("(p r) e -> p r e", r=CHUNKS), CHUNKS)
-        load_rows(nc, x_raw[0], x[0].rearrange("(p r) e -> p r e", r=CHUNKS), CHUNKS)
-        load_rows(nc, wk_raw, w_k.rearrange("(r p) e -> p r e", p=P), 1)
-        for b in range(1, BATCH):
-            load_rows(nc, x_raw[b], x[b].rearrange("(p r) e -> p r e", r=CHUNKS), 1)
+        wq_rows = w_q.rearrange("(p r) e -> p r e", r=CHUNKS)
+        wk_rows = w_k.rearrange("(r p) e -> p r e", p=P)
+        x_rows = [x[b].rearrange("(p r) e -> p r e", r=CHUNKS) for b in range(BATCH)]
+        for r in range(CHUNKS):
+            load_rows(nc, wq_raw, wq_rows, r, r + 1)
+            load_rows(nc, x_raw[0], x_rows[0], r, r + 1)
+        for r in range(CHUNKS):
+            load_rows(nc, wk_raw, wk_rows, r, r + 1)
+        for r in range(CHUNKS):
+            load_rows(nc, x_raw[1], x_rows[1], r, r + 1)
+        for b in range(2, BATCH):
+            load_rows(nc, x_raw[b], x_rows[b], 0, CHUNKS)
 
         identity = keep.tile([P, P], F32, name="identity")
         make_identity(nc, identity[:])
 
-        def prepare_x(b):
-            operand = mx_tiles(stage, "x", [P, CHUNKS * PASSES * P])
-            transpose_and_quantise(
-                nc, psum, stage, identity, x_raw[b], operand, nc.vector.tensor_copy
-            )
-            return operand
+        def rows_grouped():
+            return stage.tile([P, CHUNKS * MODEL], BF16, name="rows_grouped", align_bytes=64, bufs=3)
+
+        def sums_grouped(name):
+            return stage.tile([P, CHUNKS * P, PACK], BF16, name=name + "_grouped", align_bytes=64)
+
+        def quantise_sums(grouped, operand, piece, pieces):
+            quantise(nc, grouped[:].rearrange("p w t -> p (w t)"), operand, piece, pieces)
 
         wq_mx = mx_tiles(keep, "wq", [P, CHUNKS * PASSES * P])
         wk_mx = mx_tiles(keep, "wk", [P, CHUNKS * PASSES * P])
-        transpose_and_quantise(nc, psum, stage, identity, wq_raw, wq_mx, nc.scalar.copy)
-        x_mx = prepare_x(0)
-        q_grouped = project(nc, psum, stage, "q", wq_mx, x_mx)
-        transpose_and_quantise(nc, psum, stage, identity, wk_raw, wk_mx, nc.scalar.copy)
+        x_mx = mx_tiles(stage, "x", [P, CHUNKS * PASSES * P])
+
+        wq_grouped = rows_grouped()
+        x_grouped = rows_grouped()
+        wk_grouped = rows_grouped()
+        q_grouped = sums_grouped("q")
+
+        zeros = keep.tile([P, 4 * P], BF16, name="zeros")
+        nc.vector.memset(zeros[:], 0.0)
+        idle_bank = sum_bank(psum)
+
+        def keep_warm():
+            nc.tensor.matmul(
+                idle_bank[:].rearrange("p t w -> p (t w)"),
+                lhsT=zeros[:, :P],
+                rhs=zeros[:],
+                start=True,
+                stop=True,
+            )
+
+        for i in range(3):
+            keep_warm()
+        q_banks = [sum_bank(psum) for c in range(CHUNKS)]
+
+        def new_pairs(r):
+            for c in range(r):
+                project_part(nc, q_banks[c], wq_mx, x_mx, r, c)
+            for t in range(r + 1):
+                project_part(nc, q_banks[r], wq_mx, x_mx, t, r)
+
+        for r in range(CHUNKS):
+            wq_bank = turn(nc, psum, identity, wq_raw, r)
+            group_words(wq_grouped, wq_bank, r, nc.scalar.copy)
+            x_bank = turn(nc, psum, identity, x_raw[0], r)
+            group_words(x_grouped, x_bank, r, nc.vector.tensor_copy)
+            quantise(nc, wq_grouped[:], wq_mx, r, CHUNKS)
+            quantise(nc, x_grouped[:], x_mx, r, CHUNKS)
+            if r < CHUNKS // 2:
+                keep_warm()
+            if r > 0:
+                new_pairs(r - 1)
+
+        def turn_wk(r, copy):
+            group_words(wk_grouped, turn(nc, psum, identity, wk_raw, r), r, copy)
+
+        for r in (0, 1):
+            turn_wk(r, nc.scalar.copy)
+            quantise(nc, wk_grouped[:], wk_mx, r, CHUNKS)
+        new_pairs(CHUNKS - 1)
+        for c in range(CHUNKS):
+            round_sums(nc, q_grouped, q_banks[c], c)
+        for r in (2, 3):
+            turn_wk(r, nc.vector.tensor_copy)
+        for r in (2, 3):
+            quantise(nc, wk_grouped[:], wk_mx, r, CHUNKS)
+
+        def prepare_x(b):
+            operand = mx_tiles(stage, "x", [P, CHUNKS * PASSES * P])
+            grouped = rows_grouped()
+            for r in range(CHUNKS):
+                bank = turn(nc, psum, identity, x_raw[b], r)
+                group_words(grouped, bank, r, nc.vector.tensor_copy)
+                if r > 0:
+                    quantise(nc, grouped[:], operand, r - 1, CHUNKS)
+            quantise(nc, grouped[:], operand, CHUNKS - 1, CHUNKS)
+            return operand
+
+        def project(name, stationary, moving):
+            grouped = sums_grouped(name)
+            for c in range(CHUNKS):
+                project_chunk(nc, psum, grouped, stationary, moving, c)
+            return grouped
+
+        k_grouped = sums_grouped("k")
+        for c in (0, 1):
+            project_chunk(nc, psum, k_grouped, x_mx, wk_mx, c)
+        x_next = prepare_x(1)
+        for c in (2, 3):
+            project_chunk(nc, psum, k_grouped, x_mx, wk_mx, c)
 
         q_mx = None
         k_mx = None
         for b in range(BATCH):
-            x_next = prepare_x(b + 1) if b + 1 < BATCH else None
+            last = b + 1 == BATCH
+            if b > 0:
+                x_next = None if last else prepare_x(b + 1)
             q_before, k_before = q_mx, k_mx
             q_mx = mx_tiles(stage, "q", [P, TOKENS])
-            quantise(nc, q_grouped[:].rearrange("p w t -> p (w t)"), q_mx, 0, 1)
-            k_grouped = project(nc, psum, stage, "k", x_mx, wk_mx)
+            quantise_sums(q_grouped, q_mx, 0, 1)
+            if b > 0:
+                k_grouped = project("k", x_mx, wk_mx)
             k_mx = mx_tiles(stage, "k", [P, HEAD])
-            quantise(nc, k_grouped[:].rearrange("p w t -> p (w t)"), k_mx, 0, 1)
+            pieces = CHUNKS if last else 1
+            for piece in range(pieces):
+                quantise_sums(k_grouped, k_mx, piece, pieces)
             if b > 0:
                 logits(nc, psum, results, q_before, k_before, out[b - 1, 0])
-            if b + 1 < BATCH:
-                q_grouped = project(nc, psum, stage, "q", wq_mx, x_next)
+            if not last:
+                q_grouped = project("q", wq_mx, x_next)
             x_mx = x_next
         logits(nc, psum, results, q_mx, k_mx, out[BATCH - 1, 0])

@@ -19,6 +19,8 @@ HALF_OF_PSUM = 4
 
 assert TOKENS == HEAD == P * PACK
 
+SCATTERED = (3, 5, 7)
+
 FLOPS = 2 * BATCH * TOKENS * MODEL * HEAD * 2 + 2 * BATCH * TOKENS * HEAD * HEAD
 
 
@@ -33,8 +35,21 @@ def load_rows(nc, raw, rows, first, end):
     nc.sync.dma_start(out=raw_chunks[:, first:end, :], in_=rows[:, first:end, :])
 
 
+def scatter_rows(nc, raw, rows):
+    rows_by_group = rows.rearrange("(R j) e -> j R e", j=16)
+    raw_groups = raw[:].rearrange("p (g R e) -> p g R e", g=PASSES, e=64)
+    for g in range(PASSES):
+        for i in range(4):
+            for u in range(2):
+                first = 512 * g + 256 * u + 64 * i
+                nc.sync.dma_start(
+                    out=raw_groups[32 * i + u : 32 * (i + 1) : 2, g, :, :],
+                    in_=rows_by_group[:, :, first : first + 64],
+                )
+
+
 def quantise(nc, grouped, operand, piece, pieces):
-    codes, scales = operand
+    codes, scales = operand[:2]
     width = grouped.shape[1] // PACK // pieces
     cols = slice(piece * width, (piece + 1) * width)
     nc.vector.quantize_mx(
@@ -60,8 +75,9 @@ def group_words(grouped, bank, r, copy):
 
 
 def mx_columns(operand, r, g):
-    codes, scales = operand
-    cols = slice((r * PASSES + g) * P, (r * PASSES + g + 1) * P)
+    codes, scales, by_pass = operand
+    block = g * CHUNKS + r if by_pass else r * PASSES + g
+    cols = slice(block * P, (block + 1) * P)
     return codes[:, cols].bitcast(FP8X4), scales[:, cols]
 
 
@@ -100,7 +116,7 @@ def project_chunk(nc, psum, grouped, stationary, moving, c):
 def logits(nc, psum, results, q, k, out_b):
     q_codes, q_scales = q
     k_codes, k_scales = k
-    out_chunks = out_b.rearrange("(p c) m -> p c m", c=CHUNKS)
+    out_chunks = out_b.rearrange("(c p) m -> p c m", p=P)
     result = results.tile([P, CHUNKS, HEAD], F32, name="result")
     for c in range(CHUNKS):
         cols = slice(c * P, (c + 1) * P)
@@ -130,10 +146,12 @@ def tile_attention_pa_t_kernel(tc, x, w_q, w_k, out):
 
         wq_raw = keep.tile([P, CHUNKS * MODEL], BF16, name="wq_raw")
         wk_raw = keep.tile([P, CHUNKS * MODEL], BF16, name="wk_raw")
-        x_raw = [keep.tile([P, CHUNKS * MODEL], BF16, name="x_raw%d" % b) for b in range(BATCH)]
-        wq_rows = w_q.rearrange("(p r) e -> p r e", r=CHUNKS)
+        x_raw = [
+            keep.tile([P, CHUNKS * MODEL], BF16, name="x_raw%d" % b, align_bytes=64) for b in range(BATCH)
+        ]
+        wq_rows = w_q.rearrange("(r p) e -> p r e", p=P)
         wk_rows = w_k.rearrange("(r p) e -> p r e", p=P)
-        x_rows = [x[b].rearrange("(p r) e -> p r e", r=CHUNKS) for b in range(BATCH)]
+        x_rows = [x[b].rearrange("(r p) e -> p r e", p=P) for b in range(BATCH)]
         for r in range(CHUNKS):
             load_rows(nc, wq_raw, wq_rows, r, r + 1)
             load_rows(nc, x_raw[0], x_rows[0], r, r + 1)
@@ -141,8 +159,15 @@ def tile_attention_pa_t_kernel(tc, x, w_q, w_k, out):
             load_rows(nc, wk_raw, wk_rows, r, r + 1)
         for r in range(CHUNKS):
             load_rows(nc, x_raw[1], x_rows[1], r, r + 1)
-        for b in range(2, BATCH):
-            load_rows(nc, x_raw[b], x_rows[b], 0, CHUNKS)
+
+        def load_x(b):
+            if b in SCATTERED:
+                scatter_rows(nc, x_raw[b], x[b])
+            else:
+                load_rows(nc, x_raw[b], x_rows[b], 0, CHUNKS)
+
+        for b in (2, 3):
+            load_x(b)
 
         identity = keep.tile([P, P], F32, name="identity")
         make_identity(nc, identity[:])
@@ -156,9 +181,9 @@ def tile_attention_pa_t_kernel(tc, x, w_q, w_k, out):
         def quantise_sums(grouped, operand, piece, pieces):
             quantise(nc, grouped[:].rearrange("p w t -> p (w t)"), operand, piece, pieces)
 
-        wq_mx = mx_tiles(keep, "wq", [P, CHUNKS * PASSES * P])
-        wk_mx = mx_tiles(keep, "wk", [P, CHUNKS * PASSES * P])
-        x_mx = mx_tiles(stage, "x", [P, CHUNKS * PASSES * P])
+        wq_mx = mx_tiles(keep, "wq", [P, CHUNKS * PASSES * P]) + (False,)
+        wk_mx = mx_tiles(keep, "wk", [P, CHUNKS * PASSES * P]) + (False,)
+        x_mx = mx_tiles(stage, "x", [P, CHUNKS * PASSES * P]) + (False,)
 
         wq_grouped = rows_grouped()
         x_grouped = rows_grouped()
@@ -215,8 +240,18 @@ def tile_attention_pa_t_kernel(tc, x, w_q, w_k, out):
             quantise(nc, wk_grouped[:], wk_mx, r, CHUNKS)
 
         def prepare_x(b):
-            operand = mx_tiles(stage, "x", [P, CHUNKS * PASSES * P])
+            operand = mx_tiles(stage, "x", [P, CHUNKS * PASSES * P]) + (b in SCATTERED,)
             grouped = rows_grouped()
+            if b in SCATTERED:
+                words = CHUNKS * MODEL // 2 // PASSES
+                for g in range(PASSES):
+                    cols = slice(g * words, (g + 1) * words)
+                    nc.vector.transpose(
+                        out=grouped[:].bitcast(F32)[:, cols], in_=x_raw[b][:].bitcast(F32)[:, cols]
+                    )
+                for g in range(PASSES):
+                    quantise(nc, grouped[:], operand, g, PASSES)
+                return operand
             for r in range(CHUNKS):
                 bank = turn(nc, psum, identity, x_raw[b], r)
                 group_words(grouped, bank, r, nc.vector.tensor_copy)
@@ -242,6 +277,8 @@ def tile_attention_pa_t_kernel(tc, x, w_q, w_k, out):
         k_mx = None
         for b in range(BATCH):
             last = b + 1 == BATCH
+            if b + 4 < BATCH:
+                load_x(b + 4)
             if b > 0:
                 x_next = None if last else prepare_x(b + 1)
             q_before, k_before = q_mx, k_mx

@@ -113,7 +113,7 @@ def project_chunk(nc, psum, grouped, stationary, moving, c):
     round_sums(nc, grouped, bank, c)
 
 
-def logits(nc, psum, results, q, k, out_b):
+def logits(nc, psum, results, q, k, out_b, by_vector):
     q_codes, q_scales = q
     k_codes, k_scales = k
     out_chunks = out_b.rearrange("(c p) m -> p c m", p=P)
@@ -130,7 +130,7 @@ def logits(nc, psum, results, q, k, out_b):
             start=True,
             stop=True,
         )
-        copy = nc.scalar.copy if c % 2 == 0 else nc.vector.tensor_copy
+        copy = nc.vector.tensor_copy if c in by_vector else nc.scalar.copy
         copy(out=result[:, c, :], in_=bank[:])
         nc.sync.dma_start(out=out_chunks[:, c, :], in_=result[:, c, :])
 
@@ -291,8 +291,9 @@ def tile_attention_pa_t_kernel(tc, x, w_q, w_k, out):
             for piece in range(pieces):
                 quantise_sums(k_grouped, k_mx, piece, pieces)
             if b > 0:
-                logits(nc, psum, results, q_before, k_before, out[b - 1, 0])
+                by_vector = (3,) if b + 1 in SCATTERED else (1, 3)
+                logits(nc, psum, results, q_before, k_before, out[b - 1, 0], by_vector)
             if not last:
                 q_grouped = project("q", wq_mx, x_next)
             x_mx = x_next
-        logits(nc, psum, results, q_mx, k_mx, out[BATCH - 1, 0])
+        logits(nc, psum, results, q_mx, k_mx, out[BATCH - 1, 0], (1, 3))

@@ -19,7 +19,7 @@ HALF_OF_PSUM = 4
 
 assert TOKENS == HEAD == P * PACK
 
-SCATTERED = (3, 5, 7)
+SCATTERED = (3, 5, 6, 7)
 
 FLOPS = 2 * BATCH * TOKENS * MODEL * HEAD * 2 + 2 * BATCH * TOKENS * HEAD * HEAD
 
@@ -113,7 +113,7 @@ def project_chunk(nc, psum, grouped, stationary, moving, c):
     round_sums(nc, grouped, bank, c)
 
 
-def logits(nc, psum, results, q, k, out_b, by_vector):
+def logits(nc, psum, results, q, k, out_b):
     q_codes, q_scales = q
     k_codes, k_scales = k
     out_chunks = out_b.rearrange("(c p) m -> p c m", p=P)
@@ -130,9 +130,36 @@ def logits(nc, psum, results, q, k, out_b, by_vector):
             start=True,
             stop=True,
         )
-        copy = nc.vector.tensor_copy if c in by_vector else nc.scalar.copy
+        copy = nc.scalar.copy if c % 2 == 0 else nc.vector.tensor_copy
         copy(out=result[:, c, :], in_=bank[:])
         nc.sync.dma_start(out=out_chunks[:, c, :], in_=result[:, c, :])
+
+
+def last_logits(nc, psum, results, q, k, out_b):
+    q_codes, q_scales = q
+    k_codes, k_scales = k
+    out_chunks = out_b.rearrange("(c p) m -> p c m", p=P)
+    half = HEAD // 2
+    for h in range(2):
+        m_cols = slice(h * half, (h + 1) * half)
+        result = results.tile([P, CHUNKS, half], F32, name="half_result", bufs=2)
+        for c in range(CHUNKS):
+            cols = slice(c * P, (c + 1) * P)
+            bank = psum.tile(
+                [P, half], F32, tag=("turned", "sums")[h], name="half_logits", bufs=HALF_OF_PSUM
+            )
+            nc.tensor.matmul_mx(
+                out=bank[:],
+                lhsT=q_codes[:, cols].bitcast(FP8X4),
+                lhsT_scale=q_scales[:, cols],
+                rhs=k_codes[:, m_cols].bitcast(FP8X4),
+                rhs_scale=k_scales[:, m_cols],
+                start=True,
+                stop=True,
+            )
+            copy = nc.scalar.copy if c % 2 == 0 else nc.vector.tensor_copy
+            copy(out=result[:, c, :], in_=bank[:])
+            nc.sync.dma_start(out=out_chunks[:, c, m_cols], in_=result[:, c, :])
 
 
 def tile_attention_pa_t_kernel(tc, x, w_q, w_k, out):
@@ -228,16 +255,14 @@ def tile_attention_pa_t_kernel(tc, x, w_q, w_k, out):
         def turn_wk(r, copy):
             group_words(wk_grouped, turn(nc, psum, identity, wk_raw, r), r, copy)
 
-        for r in (0, 1):
-            turn_wk(r, nc.scalar.copy)
-            quantise(nc, wk_grouped[:], wk_mx, r, CHUNKS)
+        for r in range(CHUNKS):
+            turn_wk(r, nc.scalar.copy if r % 2 == 0 else nc.vector.tensor_copy)
+            if r > 0:
+                quantise(nc, wk_grouped[:], wk_mx, r - 1, CHUNKS)
+        quantise(nc, wk_grouped[:], wk_mx, CHUNKS - 1, CHUNKS)
         new_pairs(CHUNKS - 1)
         for c in range(CHUNKS):
             round_sums(nc, q_grouped, q_banks[c], c)
-        for r in (2, 3):
-            turn_wk(r, nc.vector.tensor_copy)
-        for r in (2, 3):
-            quantise(nc, wk_grouped[:], wk_mx, r, CHUNKS)
 
         def prepare_x(b):
             operand = mx_tiles(stage, "x", [P, CHUNKS * PASSES * P]) + (b in SCATTERED,)
@@ -266,34 +291,33 @@ def tile_attention_pa_t_kernel(tc, x, w_q, w_k, out):
                 project_chunk(nc, psum, grouped, stationary, moving, c)
             return grouped
 
-        k_grouped = sums_grouped("k")
-        for c in (0, 1):
-            project_chunk(nc, psum, k_grouped, x_mx, wk_mx, c)
         x_next = prepare_x(1)
-        for c in (2, 3):
-            project_chunk(nc, psum, k_grouped, x_mx, wk_mx, c)
+        k_grouped = project("k", x_mx, wk_mx)
 
         q_mx = None
         k_mx = None
-        for b in range(BATCH):
-            last = b + 1 == BATCH
+        for b in range(BATCH - 1):
             if b + 4 < BATCH:
                 load_x(b + 4)
             if b > 0:
-                x_next = None if last else prepare_x(b + 1)
+                x_next = prepare_x(b + 1)
             q_before, k_before = q_mx, k_mx
             q_mx = mx_tiles(stage, "q", [P, TOKENS])
             quantise_sums(q_grouped, q_mx, 0, 1)
             if b > 0:
                 k_grouped = project("k", x_mx, wk_mx)
             k_mx = mx_tiles(stage, "k", [P, HEAD])
-            pieces = CHUNKS if last else 1
-            for piece in range(pieces):
-                quantise_sums(k_grouped, k_mx, piece, pieces)
+            quantise_sums(k_grouped, k_mx, 0, 1)
             if b > 0:
-                by_vector = (3,) if b + 1 in SCATTERED else (1, 3)
-                logits(nc, psum, results, q_before, k_before, out[b - 1, 0], by_vector)
-            if not last:
-                q_grouped = project("q", wq_mx, x_next)
+                logits(nc, psum, results, q_before, k_before, out[b - 1, 0])
+            q_grouped = project("q", wq_mx, x_next)
             x_mx = x_next
-        logits(nc, psum, results, q_mx, k_mx, out[BATCH - 1, 0], (1, 3))
+        logits(nc, psum, results, q_mx, k_mx, out[BATCH - 2, 0])
+        q_mx = mx_tiles(stage, "q", [P, TOKENS])
+        quantise_sums(q_grouped, q_mx, 0, 1)
+        k_grouped = project("k", x_mx, wk_mx)
+        k_mx = mx_tiles(stage, "k", [P, HEAD])
+        quantise_sums(k_grouped, k_mx, 0, 2)
+        for c in (2, 3):
+            quantise_sums(k_grouped, k_mx, c, CHUNKS)
+        last_logits(nc, psum, results, q_mx, k_mx, out[BATCH - 1, 0])

@@ -19,7 +19,7 @@ HALF_OF_PSUM = 4
 
 assert TOKENS == HEAD == P * PACK
 
-SCATTERED = (3, 5, 6, 7)
+SCATTERED = (3, 5, 7)
 
 FLOPS = 2 * BATCH * TOKENS * MODEL * HEAD * 2 + 2 * BATCH * TOKENS * HEAD * HEAD
 
@@ -113,53 +113,33 @@ def project_chunk(nc, psum, grouped, stationary, moving, c):
     round_sums(nc, grouped, bank, c)
 
 
-def logits(nc, psum, results, q, k, out_b):
+def logits_chunk(nc, psum, result, q, k, out_b, c, copies):
     q_codes, q_scales = q
     k_codes, k_scales = k
-    out_chunks = out_b.rearrange("(c p) m -> p c m", p=P)
-    result = results.tile([P, CHUNKS, HEAD], F32, name="result")
-    for c in range(CHUNKS):
-        cols = slice(c * P, (c + 1) * P)
+    cols = slice(c * P, (c + 1) * P)
+    width = HEAD // len(copies)
+    for i, copy in enumerate(copies):
+        m_cols = slice(i * width, (i + 1) * width)
         bank = psum.tile([P, HEAD], F32, tag="turned", name="logit_bank", bufs=HALF_OF_PSUM)
         nc.tensor.matmul_mx(
-            out=bank[:],
+            out=bank[:, :width],
             lhsT=q_codes[:, cols].bitcast(FP8X4),
             lhsT_scale=q_scales[:, cols],
-            rhs=k_codes[:].bitcast(FP8X4),
-            rhs_scale=k_scales[:],
+            rhs=k_codes[:, m_cols].bitcast(FP8X4),
+            rhs_scale=k_scales[:, m_cols],
             start=True,
             stop=True,
         )
-        copy = nc.scalar.copy if c % 2 == 0 else nc.vector.tensor_copy
-        copy(out=result[:, c, :], in_=bank[:])
-        nc.sync.dma_start(out=out_chunks[:, c, :], in_=result[:, c, :])
-
-
-def last_logits(nc, psum, results, q, k, out_b):
-    q_codes, q_scales = q
-    k_codes, k_scales = k
+        copy(out=result[:, c, m_cols], in_=bank[:, :width])
     out_chunks = out_b.rearrange("(c p) m -> p c m", p=P)
-    half = HEAD // 2
-    for h in range(2):
-        m_cols = slice(h * half, (h + 1) * half)
-        result = results.tile([P, CHUNKS, half], F32, name="half_result", bufs=2)
-        for c in range(CHUNKS):
-            cols = slice(c * P, (c + 1) * P)
-            bank = psum.tile(
-                [P, half], F32, tag=("turned", "sums")[h], name="half_logits", bufs=HALF_OF_PSUM
-            )
-            nc.tensor.matmul_mx(
-                out=bank[:],
-                lhsT=q_codes[:, cols].bitcast(FP8X4),
-                lhsT_scale=q_scales[:, cols],
-                rhs=k_codes[:, m_cols].bitcast(FP8X4),
-                rhs_scale=k_scales[:, m_cols],
-                start=True,
-                stop=True,
-            )
-            copy = nc.scalar.copy if c % 2 == 0 else nc.vector.tensor_copy
-            copy(out=result[:, c, :], in_=bank[:])
-            nc.sync.dma_start(out=out_chunks[:, c, m_cols], in_=result[:, c, :])
+    nc.sync.dma_start(out=out_chunks[:, c, :], in_=result[:, c, :])
+
+
+def logits(nc, psum, results, q, k, out_b):
+    result = results.tile([P, CHUNKS, HEAD], F32, name="result")
+    for c in range(CHUNKS):
+        copy = nc.scalar.copy if c % 2 == 0 else nc.vector.tensor_copy
+        logits_chunk(nc, psum, result, q, k, out_b, c, (copy,))
 
 
 def tile_attention_pa_t_kernel(tc, x, w_q, w_k, out):
@@ -296,6 +276,11 @@ def tile_attention_pa_t_kernel(tc, x, w_q, w_k, out):
 
         q_mx = None
         k_mx = None
+        def quantised_k(k_grouped):
+            operand = mx_tiles(stage, "k", [P, HEAD])
+            quantise_sums(k_grouped, operand, 0, 1)
+            return operand
+
         for b in range(BATCH - 1):
             if b + 4 < BATCH:
                 load_x(b + 4)
@@ -306,18 +291,31 @@ def tile_attention_pa_t_kernel(tc, x, w_q, w_k, out):
             quantise_sums(q_grouped, q_mx, 0, 1)
             if b > 0:
                 k_grouped = project("k", x_mx, wk_mx)
-            k_mx = mx_tiles(stage, "k", [P, HEAD])
-            quantise_sums(k_grouped, k_mx, 0, 1)
+            k_mx = quantised_k(k_grouped)
             if b > 0:
                 logits(nc, psum, results, q_before, k_before, out[b - 1, 0])
-            q_grouped = project("q", wq_mx, x_next)
+            if b + 2 < BATCH:
+                q_grouped = project("q", wq_mx, x_next)
             x_mx = x_next
-        logits(nc, psum, results, q_mx, k_mx, out[BATCH - 2, 0])
-        q_mx = mx_tiles(stage, "q", [P, TOKENS])
-        quantise_sums(q_grouped, q_mx, 0, 1)
+
         k_grouped = project("k", x_mx, wk_mx)
-        k_mx = mx_tiles(stage, "k", [P, HEAD])
-        quantise_sums(k_grouped, k_mx, 0, 2)
-        for c in (2, 3):
-            quantise_sums(k_grouped, k_mx, c, CHUNKS)
-        last_logits(nc, psum, results, q_mx, k_mx, out[BATCH - 1, 0])
+        last_k = quantised_k(k_grouped)
+        logits(nc, psum, results, q_mx, k_mx, out[BATCH - 2, 0])
+        last_q = mx_tiles(stage, "q", [P, TOKENS])
+        q_grouped = sums_grouped("q")
+        result = results.tile([P, CHUNKS, HEAD], F32, name="result")
+
+        def q_chunk(c):
+            project_chunk(nc, psum, q_grouped, wq_mx, x_mx, c)
+            quantise_sums(q_grouped, last_q, c, CHUNKS)
+
+        def last_logits(c, copies):
+            logits_chunk(nc, psum, result, last_q, last_k, out[BATCH - 1, 0], c, copies)
+
+        for c in range(3):
+            q_chunk(c)
+        last_logits(0, (nc.vector.tensor_copy,))
+        q_chunk(3)
+        last_logits(1, (nc.scalar.copy,))
+        last_logits(2, (nc.vector.tensor_copy,))
+        last_logits(3, (nc.scalar.copy, nc.vector.tensor_copy))

@@ -1,4 +1,5 @@
 from contextlib import ExitStack
+from functools import partial
 
 import concourse.mybir as mybir
 from concourse.masks import make_identity
@@ -19,7 +20,7 @@ HALF_OF_PSUM = 4
 
 assert TOKENS == HEAD == P * PACK
 
-SCATTERED = (3, 5, 7)
+SCATTERED = {3: 4, 5: 4, 6: 2, 7: 4}
 
 FLOPS = 2 * BATCH * TOKENS * MODEL * HEAD * 2 + 2 * BATCH * TOKENS * HEAD * HEAD
 
@@ -37,7 +38,7 @@ def load_rows(nc, raw, rows, first, end):
 
 def scatter_rows(nc, raw, rows):
     rows_by_group = rows.rearrange("(R j) e -> j R e", j=16)
-    raw_groups = raw[:].rearrange("p (g R e) -> p g R e", g=PASSES, e=64)
+    raw_groups = raw.rearrange("p (g R e) -> p g R e", g=PASSES, e=64)
     for g in range(PASSES):
         for i in range(4):
             for u in range(2):
@@ -75,8 +76,8 @@ def group_words(grouped, bank, r, copy):
 
 
 def mx_columns(operand, r, g):
-    codes, scales, by_pass = operand
-    block = g * CHUNKS + r if by_pass else r * PASSES + g
+    codes, scales, scattered = operand
+    block = g * scattered + r if r < scattered else r * PASSES + g
     cols = slice(block * P, (block + 1) * P)
     return codes[:, cols].bitcast(FP8X4), scales[:, cols]
 
@@ -147,7 +148,7 @@ def tile_attention_pa_t_kernel(tc, x, w_q, w_k, out):
     with ExitStack() as ctx:
         keep = ctx.enter_context(tc.tile_pool(name="keep", bufs=1))
         stage = ctx.enter_context(tc.tile_pool(name="stage", bufs=2))
-        results = ctx.enter_context(tc.tile_pool(name="results", bufs=3))
+        results = ctx.enter_context(tc.tile_pool(name="results", bufs=4))
         psum = ctx.enter_context(tc.psum_pool(name="psum", bufs=1))
         ctx.enter_context(tc.manual_schedule())
 
@@ -168,12 +169,13 @@ def tile_attention_pa_t_kernel(tc, x, w_q, w_k, out):
             load_rows(nc, x_raw[1], x_rows[1], r, r + 1)
 
         def load_x(b):
-            if b in SCATTERED:
-                scatter_rows(nc, x_raw[b], x[b])
-            else:
-                load_rows(nc, x_raw[b], x_rows[b], 0, CHUNKS)
+            scattered = SCATTERED.get(b, 0)
+            if scattered > 0:
+                scatter_rows(nc, x_raw[b][:, : scattered * MODEL], x[b][: scattered * P])
+            if scattered < CHUNKS:
+                load_rows(nc, x_raw[b], x_rows[b], scattered, CHUNKS)
 
-        for b in (2, 3):
+        for b in range(2, 5):
             load_x(b)
 
         identity = keep.tile([P, P], F32, name="identity")
@@ -188,9 +190,9 @@ def tile_attention_pa_t_kernel(tc, x, w_q, w_k, out):
         def quantise_sums(grouped, operand, piece, pieces):
             quantise(nc, grouped[:].rearrange("p w t -> p (w t)"), operand, piece, pieces)
 
-        wq_mx = mx_tiles(keep, "wq", [P, CHUNKS * PASSES * P]) + (False,)
-        wk_mx = mx_tiles(keep, "wk", [P, CHUNKS * PASSES * P]) + (False,)
-        x_mx = mx_tiles(stage, "x", [P, CHUNKS * PASSES * P]) + (False,)
+        wq_mx = mx_tiles(keep, "wq", [P, CHUNKS * PASSES * P]) + (0,)
+        wk_mx = mx_tiles(keep, "wk", [P, CHUNKS * PASSES * P]) + (0,)
+        x_mx = mx_tiles(stage, "x", [P, CHUNKS * PASSES * P]) + (0,)
 
         wq_grouped = rows_grouped()
         x_grouped = rows_grouped()
@@ -245,24 +247,39 @@ def tile_attention_pa_t_kernel(tc, x, w_q, w_k, out):
             round_sums(nc, q_grouped, q_banks[c], c)
 
         def prepare_x(b):
-            operand = mx_tiles(stage, "x", [P, CHUNKS * PASSES * P]) + (b in SCATTERED,)
+            scattered = SCATTERED.get(b, 0)
+            operand = mx_tiles(stage, "x", [P, CHUNKS * PASSES * P]) + (scattered,)
             grouped = rows_grouped()
-            if b in SCATTERED:
-                words = CHUNKS * MODEL // 2 // PASSES
-                for g in range(PASSES):
-                    cols = slice(g * words, (g + 1) * words)
-                    nc.vector.transpose(
-                        out=grouped[:].bitcast(F32)[:, cols], in_=x_raw[b][:].bitcast(F32)[:, cols]
-                    )
-                for g in range(PASSES):
-                    quantise(nc, grouped[:], operand, g, PASSES)
-                return operand
-            for r in range(CHUNKS):
+            words = scattered * MODEL // 2 // PASSES
+
+            def turn_blocks(g):
+                cols = slice(g * words, (g + 1) * words)
+                nc.vector.transpose(
+                    out=grouped[:].bitcast(F32)[:, cols], in_=x_raw[b][:].bitcast(F32)[:, cols]
+                )
+
+            def turn_chunk(r):
                 bank = turn(nc, psum, identity, x_raw[b], r)
                 group_words(grouped, bank, r, nc.vector.tensor_copy)
-                if r > 0:
-                    quantise(nc, grouped[:], operand, r - 1, CHUNKS)
-            quantise(nc, grouped[:], operand, CHUNKS - 1, CHUNKS)
+
+            def quantise_part(piece, pieces):
+                quantise(nc, grouped[:], operand, piece, pieces)
+
+            parts = []
+            if scattered > 0:
+                pieces = PASSES * CHUNKS // scattered
+                parts += [(partial(turn_blocks, g), partial(quantise_part, g, pieces)) for g in range(PASSES)]
+            parts += [
+                (partial(turn_chunk, r), partial(quantise_part, r, CHUNKS))
+                for r in range(scattered, CHUNKS)
+            ]
+            late = None
+            for make, pack in parts:
+                make()
+                if late:
+                    late()
+                late = pack
+            late()
             return operand
 
         def project(name, stationary, moving):
@@ -282,8 +299,8 @@ def tile_attention_pa_t_kernel(tc, x, w_q, w_k, out):
             return operand
 
         for b in range(BATCH - 1):
-            if b + 4 < BATCH:
-                load_x(b + 4)
+            if b + 5 < BATCH:
+                load_x(b + 5)
             if b > 0:
                 x_next = prepare_x(b + 1)
             q_before, k_before = q_mx, k_mx

from contextlib import ExitStack
from functools import partial

import concourse.mybir as mybir
from concourse.masks import make_identity

BF16 = mybir.dt.bfloat16
F32 = mybir.dt.float32
U32 = mybir.dt.uint32
U8 = mybir.dt.uint8
FP8X4 = mybir.dt.float8_e4m3fn_x4

P = 128
PACK = 4
BATCH, TOKENS, MODEL, HEAD = 8, 512, 1024, 512
CHUNKS = TOKENS // P
PASSES = MODEL // (P * PACK)
WORD_CHUNKS = MODEL // 2 // P
HALF_OF_PSUM = 4

assert TOKENS == HEAD == P * PACK

SCATTERED = {3: 4, 5: 4, 6: 2, 7: 4}

FLOPS = 2 * BATCH * TOKENS * MODEL * HEAD * 2 + 2 * BATCH * TOKENS * HEAD * HEAD


def mx_tiles(pool, name, shape):
    codes = pool.tile(shape, U32, name=name + "_codes", align_bytes=64)
    scales = pool.tile(shape, U8, name=name + "_scales", align_bytes=64)
    return codes, scales


def load_rows(nc, raw, rows, first, end):
    raw_chunks = raw[:].rearrange("p (r e) -> p r e", r=CHUNKS)
    nc.sync.dma_start(out=raw_chunks[:, first:end, :], in_=rows[:, first:end, :])


def scatter_rows(nc, raw, rows):
    rows_by_group = rows.rearrange("(R j) e -> j R e", j=16)
    raw_groups = raw.rearrange("p (g R e) -> p g R e", g=PASSES, e=64)
    for g in range(PASSES):
        for i in range(4):
            for u in range(2):
                first = 512 * g + 256 * u + 64 * i
                nc.sync.dma_start(
                    out=raw_groups[32 * i + u : 32 * (i + 1) : 2, g, :, :],
                    in_=rows_by_group[:, :, first : first + 64],
                )


def quantise(nc, grouped, operand, piece, pieces):
    codes, scales = operand[:2]
    width = grouped.shape[1] // PACK // pieces
    cols = slice(piece * width, (piece + 1) * width)
    nc.vector.quantize_mx(
        out=codes[:, cols].bitcast(FP8X4),
        scales=scales[:, cols],
        in_=grouped[:, piece * width * PACK : (piece + 1) * width * PACK],
    )


def turn(nc, psum, identity, raw, r):
    raw_words = raw[:].bitcast(F32).rearrange("p (r s v) -> p r s v", r=CHUNKS, s=WORD_CHUNKS)
    bank = psum.tile([P, WORD_CHUNKS, P], F32, tag="turned", name="turned", bufs=HALF_OF_PSUM)
    for s in range(WORD_CHUNKS):
        nc.tensor.transpose(bank[:, s, :], raw_words[:, r, s, :], identity[:])
    return bank


def group_words(grouped, bank, r, copy):
    grouped_words = grouped[:].bitcast(F32).rearrange(
        "p (r g c u) -> p r g c u", r=CHUNKS, g=PASSES, u=2
    )
    copy(out=grouped_words[:, r], in_=bank[:].rearrange("p (g u) c -> p g c u", u=2))


def mx_columns(operand, r, g):
    codes, scales, scattered = operand
    block = g * scattered + r if r < scattered else r * PASSES + g
    cols = slice(block * P, (block + 1) * P)
    return codes[:, cols].bitcast(FP8X4), scales[:, cols]


def sum_bank(psum):
    return psum.tile([P, PACK, P], F32, tag="sums", name="sums", bufs=HALF_OF_PSUM)


def project_part(nc, bank, stationary, moving, t, c):
    for g in range(PASSES):
        lhsT, lhsT_scale = mx_columns(stationary, t, g)
        rhs, rhs_scale = mx_columns(moving, c, g)
        nc.tensor.matmul_mx(
            out=bank[:, t, :],
            lhsT=lhsT,
            lhsT_scale=lhsT_scale,
            rhs=rhs,
            rhs_scale=rhs_scale,
            start=(g == 0),
            stop=(g == PASSES - 1),
        )


def round_sums(nc, grouped, bank, c):
    nc.scalar.copy(
        out=grouped[:, c * P : (c + 1) * P, :], in_=bank[:].rearrange("p t w -> p w t")
    )


def project_chunk(nc, psum, grouped, stationary, moving, c):
    bank = sum_bank(psum)
    for t in range(PACK):
        project_part(nc, bank, stationary, moving, t, c)
    round_sums(nc, grouped, bank, c)


def logits_chunk(nc, psum, result, q, k, out_b, c, copies):
    q_codes, q_scales = q
    k_codes, k_scales = k
    cols = slice(c * P, (c + 1) * P)
    width = HEAD // len(copies)
    for i, copy in enumerate(copies):
        m_cols = slice(i * width, (i + 1) * width)
        bank = psum.tile([P, HEAD], F32, tag="turned", name="logit_bank", bufs=HALF_OF_PSUM)
        nc.tensor.matmul_mx(
            out=bank[:, :width],
            lhsT=q_codes[:, cols].bitcast(FP8X4),
            lhsT_scale=q_scales[:, cols],
            rhs=k_codes[:, m_cols].bitcast(FP8X4),
            rhs_scale=k_scales[:, m_cols],
            start=True,
            stop=True,
        )
        copy(out=result[:, c, m_cols], in_=bank[:, :width])
    out_chunks = out_b.rearrange("(c p) m -> p c m", p=P)
    nc.sync.dma_start(out=out_chunks[:, c, :], in_=result[:, c, :])


def logits(nc, psum, results, q, k, out_b):
    result = results.tile([P, CHUNKS, HEAD], F32, name="result")
    for c in range(CHUNKS):
        copy = nc.scalar.copy if c % 2 == 0 else nc.vector.tensor_copy
        logits_chunk(nc, psum, result, q, k, out_b, c, (copy,))


def tile_attention_pa_t_kernel(tc, x, w_q, w_k, out):
    nc = tc.nc
    with ExitStack() as ctx:
        keep = ctx.enter_context(tc.tile_pool(name="keep", bufs=1))
        stage = ctx.enter_context(tc.tile_pool(name="stage", bufs=2))
        results = ctx.enter_context(tc.tile_pool(name="results", bufs=4))
        psum = ctx.enter_context(tc.psum_pool(name="psum", bufs=1))
        ctx.enter_context(tc.manual_schedule())

        wq_raw = keep.tile([P, CHUNKS * MODEL], BF16, name="wq_raw")
        wk_raw = keep.tile([P, CHUNKS * MODEL], BF16, name="wk_raw")
        x_raw = [
            keep.tile([P, CHUNKS * MODEL], BF16, name="x_raw%d" % b, align_bytes=64) for b in range(BATCH)
        ]
        wq_rows = w_q.rearrange("(r p) e -> p r e", p=P)
        wk_rows = w_k.rearrange("(r p) e -> p r e", p=P)
        x_rows = [x[b].rearrange("(r p) e -> p r e", p=P) for b in range(BATCH)]
        for r in range(CHUNKS):
            load_rows(nc, wq_raw, wq_rows, r, r + 1)
            load_rows(nc, x_raw[0], x_rows[0], r, r + 1)
        for r in range(CHUNKS):
            load_rows(nc, wk_raw, wk_rows, r, r + 1)
        for r in range(CHUNKS):
            load_rows(nc, x_raw[1], x_rows[1], r, r + 1)

        def load_x(b):
            scattered = SCATTERED.get(b, 0)
            if scattered > 0:
                scatter_rows(nc, x_raw[b][:, : scattered * MODEL], x[b][: scattered * P])
            if scattered < CHUNKS:
                load_rows(nc, x_raw[b], x_rows[b], scattered, CHUNKS)

        for b in range(2, 5):
            load_x(b)

        identity = keep.tile([P, P], F32, name="identity")
        make_identity(nc, identity[:])

        def rows_grouped():
            return stage.tile([P, CHUNKS * MODEL], BF16, name="rows_grouped", align_bytes=64, bufs=3)

        def sums_grouped(name):
            return stage.tile([P, CHUNKS * P, PACK], BF16, name=name + "_grouped", align_bytes=64)

        def quantise_sums(grouped, operand, piece, pieces):
            quantise(nc, grouped[:].rearrange("p w t -> p (w t)"), operand, piece, pieces)

        wq_mx = mx_tiles(keep, "wq", [P, CHUNKS * PASSES * P]) + (0,)
        wk_mx = mx_tiles(keep, "wk", [P, CHUNKS * PASSES * P]) + (0,)
        x_mx = mx_tiles(stage, "x", [P, CHUNKS * PASSES * P]) + (0,)

        wq_grouped = rows_grouped()
        x_grouped = rows_grouped()
        wk_grouped = rows_grouped()
        q_grouped = sums_grouped("q")

        zeros = keep.tile([P, 4 * P], BF16, name="zeros")
        nc.vector.memset(zeros[:], 0.0)
        idle_bank = sum_bank(psum)

        def keep_warm():
            nc.tensor.matmul(
                idle_bank[:].rearrange("p t w -> p (t w)"),
                lhsT=zeros[:, :P],
                rhs=zeros[:],
                start=True,
                stop=True,
            )

        for i in range(3):
            keep_warm()
        q_banks = [sum_bank(psum) for c in range(CHUNKS)]

        def new_pairs(r):
            for c in range(r):
                project_part(nc, q_banks[c], wq_mx, x_mx, r, c)
            for t in range(r + 1):
                project_part(nc, q_banks[r], wq_mx, x_mx, t, r)

        for r in range(CHUNKS):
            wq_bank = turn(nc, psum, identity, wq_raw, r)
            group_words(wq_grouped, wq_bank, r, nc.scalar.copy)
            x_bank = turn(nc, psum, identity, x_raw[0], r)
            group_words(x_grouped, x_bank, r, nc.vector.tensor_copy)
            quantise(nc, wq_grouped[:], wq_mx, r, CHUNKS)
            quantise(nc, x_grouped[:], x_mx, r, CHUNKS)
            if r < CHUNKS // 2:
                keep_warm()
            if r > 0:
                new_pairs(r - 1)

        def turn_wk(r, copy):
            group_words(wk_grouped, turn(nc, psum, identity, wk_raw, r), r, copy)

        for r in range(CHUNKS):
            turn_wk(r, nc.scalar.copy if r % 2 == 0 else nc.vector.tensor_copy)
            if r > 0:
                quantise(nc, wk_grouped[:], wk_mx, r - 1, CHUNKS)
        quantise(nc, wk_grouped[:], wk_mx, CHUNKS - 1, CHUNKS)
        new_pairs(CHUNKS - 1)
        for c in range(CHUNKS):
            round_sums(nc, q_grouped, q_banks[c], c)

        def prepare_x(b):
            scattered = SCATTERED.get(b, 0)
            operand = mx_tiles(stage, "x", [P, CHUNKS * PASSES * P]) + (scattered,)
            grouped = rows_grouped()
            words = scattered * MODEL // 2 // PASSES

            def turn_blocks(g):
                cols = slice(g * words, (g + 1) * words)
                nc.vector.transpose(
                    out=grouped[:].bitcast(F32)[:, cols], in_=x_raw[b][:].bitcast(F32)[:, cols]
                )

            def turn_chunk(r):
                bank = turn(nc, psum, identity, x_raw[b], r)
                group_words(grouped, bank, r, nc.vector.tensor_copy)

            def quantise_part(piece, pieces):
                quantise(nc, grouped[:], operand, piece, pieces)

            parts = []
            if scattered > 0:
                pieces = PASSES * CHUNKS // scattered
                parts += [(partial(turn_blocks, g), partial(quantise_part, g, pieces)) for g in range(PASSES)]
            parts += [
                (partial(turn_chunk, r), partial(quantise_part, r, CHUNKS))
                for r in range(scattered, CHUNKS)
            ]
            late = None
            for make, pack in parts:
                make()
                if late:
                    late()
                late = pack
            late()
            return operand

        def project(name, stationary, moving):
            grouped = sums_grouped(name)
            for c in range(CHUNKS):
                project_chunk(nc, psum, grouped, stationary, moving, c)
            return grouped

        x_next = prepare_x(1)
        k_grouped = project("k", x_mx, wk_mx)

        q_mx = None
        k_mx = None
        def quantised_k(k_grouped):
            operand = mx_tiles(stage, "k", [P, HEAD])
            quantise_sums(k_grouped, operand, 0, 1)
            return operand

        for b in range(BATCH - 1):
            if b + 5 < BATCH:
                load_x(b + 5)
            if b > 0:
                x_next = prepare_x(b + 1)
            q_before, k_before = q_mx, k_mx
            q_mx = mx_tiles(stage, "q", [P, TOKENS])
            quantise_sums(q_grouped, q_mx, 0, 1)
            if b > 0:
                k_grouped = project("k", x_mx, wk_mx)
            k_mx = quantised_k(k_grouped)
            if b > 0:
                logits(nc, psum, results, q_before, k_before, out[b - 1, 0])
            if b + 2 < BATCH:
                q_grouped = project("q", wq_mx, x_next)
            x_mx = x_next

        k_grouped = project("k", x_mx, wk_mx)
        last_k = quantised_k(k_grouped)
        logits(nc, psum, results, q_mx, k_mx, out[BATCH - 2, 0])
        last_q = mx_tiles(stage, "q", [P, TOKENS])
        q_grouped = sums_grouped("q")
        result = results.tile([P, CHUNKS, HEAD], F32, name="result")

        def q_chunk(c):
            project_chunk(nc, psum, q_grouped, wq_mx, x_mx, c)
            quantise_sums(q_grouped, last_q, c, CHUNKS)

        def last_logits(c, copies):
            logits_chunk(nc, psum, result, last_q, last_k, out[BATCH - 1, 0], c, copies)

        for c in range(3):
            q_chunk(c)
        last_logits(0, (nc.vector.tensor_copy,))
        q_chunk(3)
        last_logits(1, (nc.scalar.copy,))
        last_logits(2, (nc.vector.tensor_copy,))
        last_logits(3, (nc.scalar.copy, nc.vector.tensor_copy))
